import numpy as np
import ml_dtypes

BF16 = ml_dtypes.bfloat16


def bf(x):
    return np.asarray(x, np.float32).astype(BF16)


def f32(x):
    return np.asarray(x, np.float32)


def f64(x):
    return np.asarray(x).astype(np.float64)


def striped(idx):
    return np.tile(idx.reshape(-1, 16).T, (8, 1))


R, HKV, G, D, S, L, NS, C, N, HQ = 4, 2, 256, 128, 4096, 2048, 32, 512, 8192, 512


def setup_inputs():
    idx = np.concatenate([np.random.permutation(S)[:L] for _ in range(R)])
    return {"q": bf(np.random.standard_normal((D, HQ))), "kv": f32(np.random.standard_normal((R, C, S))), "offs": striped(idx)}


def reference(q, kv, offs):
    idx = offs[:16].T.reshape(-1)
    qh = f64(q).reshape(D, HKV, G).transpose(1, 2, 0)
    kv64 = f64(kv)
    num = np.zeros((HKV, G, D))
    den = np.zeros((HKV, G, 1))
    for r in range(R):
        pick = kv64[r][:, idx[r * L:(r + 1) * L]]
        kT = pick[:HKV * D].reshape(HKV, D, L)
        vT = pick[HKV * D:].reshape(HKV, D, L)
        e = np.exp((qh @ kT) * D ** -0.5)
        z = e.reshape(HKV, G, NS, L // NS).sum(axis=-1)
        zsum = z.sum(axis=-1, keepdims=True)
        zmax = z.max(axis=-1, keepdims=True)
        num = num + (e @ vT.transpose(0, 2, 1)) * (zsum / zmax)
        den = den + zsum
    return (num / den).reshape(HQ, D)

@@ -1,0 +1,140 @@
+import math
+
+import concourse.mybir as mybir
+from concourse.masks import make_identity
+
+F32, BF16, U16 = mybir.dt.float32, mybir.dt.bfloat16, mybir.dt.uint16
+COPY, EXP = mybir.ActivationFunctionType.Copy, mybir.ActivationFunctionType.Exp
+MULT, ADD, MAX = mybir.AluOpType.mult, mybir.AluOpType.add, mybir.AluOpType.max
+X = mybir.AxisListType.X
+
+P = 128
+RANKS = 4
+KV_HEADS = 2
+GROUP = 256
+D = 128
+SLOTS = 4096
+L = 2048
+SPLITS = 32
+SPLIT = L // SPLITS
+BLOCKS = L // P
+SPLITS_IN_BLOCK = P // SPLIT
+HEAD_BLOCKS = GROUP // P
+SCORE_BLOCKS = 512 // GROUP
+FLIP_BLOCKS = 512 // D
+
+FLOPS = 2 * 2 * (KV_HEADS * GROUP) * (RANKS * L) * D
+
+
+def tile_spgqaflashdecodeiris_b_kernel(tc, q, kv, offs, out):
+    nc = tc.nc
+    out_blocks = out.rearrange("(b p) d -> p b d", p=P)
+
+    with (
+        tc.tile_pool(name="held", bufs=1) as held,
+        tc.tile_pool(name="windows", bufs=5) as windows,
+        tc.tile_pool(name="picked", bufs=3) as picked,
+        tc.tile_pool(name="operands", bufs=2) as operands,
+        tc.tile_pool(name="stats", bufs=2) as stats,
+        tc.psum_pool(name="score_banks", bufs=3) as score_banks,
+        tc.psum_pool(name="flip_banks", bufs=2) as flip_banks,
+        tc.psum_pool(name="sum_banks", bufs=2) as sum_banks,
+    ):
+        offsets = held.tile([P, RANKS * L // 16], U16, name="offsets")
+        nc.sync.dma_start(offsets[:], offs)
+        queries = held.tile([P, KV_HEADS * GROUP], BF16, name="queries")
+        nc.gpsimd.dma_start(queries[:], q)
+
+        identity = held.tile([P, P], F32, name="identity")
+        make_identity(nc, identity[:])
+
+        marks = held.tile([P, BLOCKS, SPLITS], BF16, name="marks")
+        nc.gpsimd.memset(marks[:], 0.0)
+        for b in range(BLOCKS):
+            for s in range(SPLITS_IN_BLOCK):
+                t = SPLITS_IN_BLOCK * b + s
+                nc.gpsimd.memset(marks[s * SPLIT : (s + 1) * SPLIT, b, t : t + 1], 1.0)
+
+        numerator = held.tile([P, KV_HEADS * HEAD_BLOCKS, D], F32, name="numerator")
+        denominator = held.tile([P, KV_HEADS * HEAD_BLOCKS], F32, name="denominator")
+        nc.vector.memset(numerator[:], 0.0)
+        nc.vector.memset(denominator[:], 0.0)
+
+        for r in range(RANKS):
+            rank_offsets = offsets[:, r * (L // 16) : (r + 1) * (L // 16)]
+            for a in range(KV_HEADS):
+                key_window = windows.tile([P, SLOTS], F32, tag="window")
+                nc.sync.dma_start(key_window[:], kv[r, a * D : (a + 1) * D, :])
+                value_window = windows.tile([P, SLOTS], F32, tag="window")
+                nc.sync.dma_start(value_window[:], kv[r, (KV_HEADS + a) * D : (KV_HEADS + a + 1) * D, :])
+
+                keys_f32 = picked.tile([P, L], F32, tag="picked")
+                nc.scalar.activation(keys_f32[:], key_window[:].indirect(rank_offsets), COPY)
+                keys = operands.tile([P, L], BF16, tag="keys")
+                nc.vector.tensor_copy(keys[:], keys_f32[:])
+
+                values_f32 = picked.tile([P, L], F32, tag="picked")
+                nc.scalar.activation(values_f32[:], value_window[:].indirect(rank_offsets), COPY)
+
+                values_t = operands.tile([P, BLOCKS, D + SPLITS], BF16, tag="values_t")
+                nc.vector.tensor_copy(values_t[:, :, D:], marks[:])
+                for b0 in range(0, BLOCKS, FLIP_BLOCKS):
+                    flipped = flip_banks.tile([P, FLIP_BLOCKS, D], F32, tag="flipped")
+                    for i in range(FLIP_BLOCKS):
+                        b = b0 + i
+                        nc.tensor.transpose(flipped[:, i, :], values_f32[:, b * P : (b + 1) * P], identity[:])
+                    nc.vector.tensor_copy(values_t[:, b0 : b0 + FLIP_BLOCKS, :D], flipped[:])
+
+                e_t = operands.tile([P, BLOCKS, GROUP], BF16, tag="e_t")
+                for b0 in range(0, BLOCKS, SCORE_BLOCKS):
+                    scores = score_banks.tile([P, SCORE_BLOCKS, GROUP], F32, tag="scores")
+                    for i in range(SCORE_BLOCKS):
+                        b = b0 + i
+                        nc.tensor.matmul(
+                            scores[:, i, :],
+                            keys[:, b * P : (b + 1) * P],
+                            queries[:, a * GROUP : (a + 1) * GROUP],
+                            start=True,
+                            stop=True,
+                        )
+                    nc.scalar.activation(e_t[:, b0 : b0 + SCORE_BLOCKS, :], scores[:], EXP, scale=1.0 / math.sqrt(D))
+
+                sums = sum_banks.tile([P, HEAD_BLOCKS, D + SPLITS], F32, tag="sums")
+                for g in range(HEAD_BLOCKS):
+                    for b in range(BLOCKS):
+                        nc.tensor.matmul(
+                            sums[:, g, :],
+                            e_t[:, b, g * P : (g + 1) * P],
+                            values_t[:, b, :],
+                            start=(b == 0),
+                            stop=(b == BLOCKS - 1),
+                        )
+
+                z_sum = stats.tile([P, HEAD_BLOCKS], F32, tag="z_sum")
+                nc.vector.tensor_reduce(z_sum[:], sums[:, :, D:], X, ADD)
+                z_max = stats.tile([P, HEAD_BLOCKS], F32, tag="z_max")
+                nc.vector.tensor_reduce(z_max[:], sums[:, :, D:], X, MAX)
+                weight = stats.tile([P, HEAD_BLOCKS], F32, tag="weight")
+                nc.vector.reciprocal(weight[:], z_max[:])
+                nc.vector.tensor_mul(weight[:], weight[:], z_sum[:])
+
+                first = a * HEAD_BLOCKS
+                nc.vector.tensor_add(
+                    denominator[:, first : first + HEAD_BLOCKS], denominator[:, first : first + HEAD_BLOCKS], z_sum[:]
+                )
+                for g in range(HEAD_BLOCKS):
+                    nc.vector.scalar_tensor_tensor(
+                        numerator[:, first + g, :],
+                        sums[:, g, :D],
+                        weight[:, g : g + 1],
+                        numerator[:, first + g, :],
+                        MULT,
+                        ADD,
+                    )
+
+        inverse = held.tile([P, KV_HEADS * HEAD_BLOCKS], F32, name="inverse")
+        nc.vector.reciprocal(inverse[:], denominator[:])
+        result = held.tile([P, KV_HEADS * HEAD_BLOCKS, D], F32, name="result")
+        for g in range(KV_HEADS * HEAD_BLOCKS):
+            nc.vector.tensor_scalar_mul(result[:, g, :], numerator[:, g, :], inverse[:, g : g + 1])
+        nc.sync.dma_start(out_blocks, result[:])

@@ -23,6 +23,11 @@ HEAD_BLOCKS = GROUP // P
 SCORE_BLOCKS = 512 // GROUP
 FLIP_BLOCKS = 512 // D
 
+PIECE = 1024
+PIECES = L // PIECE
+STEPS = 2 * PIECES
+STEP_BLOCKS = BLOCKS // STEPS
+
 FLOPS = 2 * 2 * (KV_HEADS * GROUP) * (RANKS * L) * D
 
 
@@ -33,108 +38,131 @@ def tile_spgqaflashdecodeiris_b_kernel(tc, q, kv, offs, out):
     with (
         tc.tile_pool(name="held", bufs=1) as held,
         tc.tile_pool(name="windows", bufs=5) as windows,
-        tc.tile_pool(name="picked", bufs=3) as picked,
-        tc.tile_pool(name="operands", bufs=2) as operands,
+        tc.tile_pool(name="picked", bufs=4) as picked,
+        tc.tile_pool(name="operands", bufs=3) as operands,
+        tc.tile_pool(name="e_pieces", bufs=6) as e_pieces,
         tc.tile_pool(name="stats", bufs=2) as stats,
-        tc.psum_pool(name="score_banks", bufs=3) as score_banks,
+        tc.psum_pool(name="score_banks", bufs=4) as score_banks,
         tc.psum_pool(name="flip_banks", bufs=2) as flip_banks,
-        tc.psum_pool(name="sum_banks", bufs=2) as sum_banks,
+        tc.psum_pool(name="sum_banks", bufs=1) as sum_banks,
     ):
         offsets = held.tile([P, RANKS * L // 16], U16, name="offsets")
         nc.sync.dma_start(offsets[:], offs)
-        queries = held.tile([P, KV_HEADS * GROUP], BF16, name="queries")
-        nc.gpsimd.dma_start(queries[:], q)
 
         identity = held.tile([P, P], F32, name="identity")
         make_identity(nc, identity[:])
 
         marks = held.tile([P, BLOCKS, SPLITS], BF16, name="marks")
-        nc.gpsimd.memset(marks[:], 0.0)
+        nc.vector.memset(marks[:], 0.0)
         for b in range(BLOCKS):
             for s in range(SPLITS_IN_BLOCK):
                 t = SPLITS_IN_BLOCK * b + s
-                nc.gpsimd.memset(marks[s * SPLIT : (s + 1) * SPLIT, b, t : t + 1], 1.0)
+                nc.vector.memset(marks[s * SPLIT : (s + 1) * SPLIT, b, t : t + 1], 1.0)
 
         numerator = held.tile([P, KV_HEADS * HEAD_BLOCKS, D], F32, name="numerator")
         denominator = held.tile([P, KV_HEADS * HEAD_BLOCKS], F32, name="denominator")
         nc.vector.memset(numerator[:], 0.0)
         nc.vector.memset(denominator[:], 0.0)
+        queries = held.tile([P, KV_HEADS * GROUP], BF16, name="queries")
 
-        for r in range(RANKS):
-            rank_offsets = offsets[:, r * (L // 16) : (r + 1) * (L // 16)]
-            for a in range(KV_HEADS):
-                key_window = windows.tile([P, SLOTS], F32, tag="window")
-                nc.sync.dma_start(key_window[:], kv[r, a * D : (a + 1) * D, :])
-                value_window = windows.tile([P, SLOTS], F32, tag="window")
-                nc.sync.dma_start(value_window[:], kv[r, (KV_HEADS + a) * D : (KV_HEADS + a + 1) * D, :])
+        def open_unit(r, a):
+            value_window = windows.tile([P, SLOTS], F32, tag="window")
+            nc.sync.dma_start(value_window[:], kv[r, (KV_HEADS + a) * D : (KV_HEADS + a + 1) * D, :])
+            key_window = windows.tile([P, SLOTS], F32, tag="window")
+            nc.sync.dma_start(key_window[:], kv[r, a * D : (a + 1) * D, :])
+            values_t = operands.tile([P, BLOCKS, D + SPLITS], BF16, tag="values_t")
+            nc.vector.tensor_copy(values_t[:, :, D:], marks[:])
+            keys = operands.tile([P, L], BF16, tag="keys")
+            return {"r": r, "a": a, "value_window": value_window, "key_window": key_window,
+                    "values_t": values_t, "keys": keys}
 
-                keys_f32 = picked.tile([P, L], F32, tag="picked")
-                nc.scalar.activation(keys_f32[:], key_window[:].indirect(rank_offsets), COPY)
-                keys = operands.tile([P, L], BF16, tag="keys")
-                nc.vector.tensor_copy(keys[:], keys_f32[:])
-
-                values_f32 = picked.tile([P, L], F32, tag="picked")
-                nc.scalar.activation(values_f32[:], value_window[:].indirect(rank_offsets), COPY)
-
-                values_t = operands.tile([P, BLOCKS, D + SPLITS], BF16, tag="values_t")
-                nc.vector.tensor_copy(values_t[:, :, D:], marks[:])
-                for b0 in range(0, BLOCKS, FLIP_BLOCKS):
+        def look_up(unit, step):
+            i = step % PIECES
+            first_column = (unit["r"] * L + i * PIECE) // 16
+            piece_offsets = offsets[:, first_column : first_column + PIECE // 16]
+            window = unit["value_window"] if step < PIECES else unit["key_window"]
+            piece = picked.tile([P, PIECE], F32, tag="piece")
+            nc.scalar.activation(piece[:], window[:].indirect(piece_offsets), COPY)
+            if step < PIECES:
+                for c0 in range(0, PIECE // P, FLIP_BLOCKS):
                     flipped = flip_banks.tile([P, FLIP_BLOCKS, D], F32, tag="flipped")
-                    for i in range(FLIP_BLOCKS):
-                        b = b0 + i
-                        nc.tensor.transpose(flipped[:, i, :], values_f32[:, b * P : (b + 1) * P], identity[:])
-                    nc.vector.tensor_copy(values_t[:, b0 : b0 + FLIP_BLOCKS, :D], flipped[:])
+                    for c in range(FLIP_BLOCKS):
+                        nc.tensor.transpose(flipped[:, c, :], piece[:, (c0 + c) * P : (c0 + c + 1) * P], identity[:])
+                    b0 = i * (PIECE // P) + c0
+                    nc.vector.tensor_copy(unit["values_t"][:, b0 : b0 + FLIP_BLOCKS, :D], flipped[:])
+            else:
+                nc.vector.tensor_copy(unit["keys"][:, i * PIECE : (i + 1) * PIECE], piece[:])
 
-                e_t = operands.tile([P, BLOCKS, GROUP], BF16, tag="e_t")
-                for b0 in range(0, BLOCKS, SCORE_BLOCKS):
-                    scores = score_banks.tile([P, SCORE_BLOCKS, GROUP], F32, tag="scores")
-                    for i in range(SCORE_BLOCKS):
-                        b = b0 + i
-                        nc.tensor.matmul(
-                            scores[:, i, :],
-                            keys[:, b * P : (b + 1) * P],
-                            queries[:, a * GROUP : (a + 1) * GROUP],
-                            start=True,
-                            stop=True,
-                        )
-                    nc.scalar.activation(e_t[:, b0 : b0 + SCORE_BLOCKS, :], scores[:], EXP, scale=1.0 / math.sqrt(D))
-
-                sums = sum_banks.tile([P, HEAD_BLOCKS, D + SPLITS], F32, tag="sums")
-                for g in range(HEAD_BLOCKS):
-                    for b in range(BLOCKS):
-                        nc.tensor.matmul(
-                            sums[:, g, :],
-                            e_t[:, b, g * P : (g + 1) * P],
-                            values_t[:, b, :],
-                            start=(b == 0),
-                            stop=(b == BLOCKS - 1),
-                        )
-
-                z_sum = stats.tile([P, HEAD_BLOCKS], F32, tag="z_sum")
-                nc.vector.tensor_reduce(z_sum[:], sums[:, :, D:], X, ADD)
-                z_max = stats.tile([P, HEAD_BLOCKS], F32, tag="z_max")
-                nc.vector.tensor_reduce(z_max[:], sums[:, :, D:], X, MAX)
-                weight = stats.tile([P, HEAD_BLOCKS], F32, tag="weight")
-                nc.vector.reciprocal(weight[:], z_max[:])
-                nc.vector.tensor_mul(weight[:], weight[:], z_sum[:])
-
-                first = a * HEAD_BLOCKS
-                nc.vector.tensor_add(
-                    denominator[:, first : first + HEAD_BLOCKS], denominator[:, first : first + HEAD_BLOCKS], z_sum[:]
-                )
-                for g in range(HEAD_BLOCKS):
-                    nc.vector.scalar_tensor_tensor(
-                        numerator[:, first + g, :],
-                        sums[:, g, :D],
-                        weight[:, g : g + 1],
-                        numerator[:, first + g, :],
-                        MULT,
-                        ADD,
+        def attend(unit, sums, step):
+            a = unit["a"]
+            for b0 in range(step * STEP_BLOCKS, (step + 1) * STEP_BLOCKS, SCORE_BLOCKS):
+                scores = score_banks.tile([P, SCORE_BLOCKS, GROUP], F32, tag="scores")
+                for i in range(SCORE_BLOCKS):
+                    nc.tensor.matmul(
+                        scores[:, i, :],
+                        unit["keys"][:, (b0 + i) * P : (b0 + i + 1) * P],
+                        queries[:, a * GROUP : (a + 1) * GROUP],
+                        start=True,
+                        stop=True,
                     )
+                e_t = e_pieces.tile([P, SCORE_BLOCKS, GROUP], BF16, tag="e_t")
+                nc.scalar.activation(e_t[:], scores[:], EXP, scale=1.0 / math.sqrt(D))
+                for i in range(SCORE_BLOCKS):
+                    for g in range(HEAD_BLOCKS):
+                        nc.tensor.matmul(
+                            sums[g][:],
+                            e_t[:, i, g * P : (g + 1) * P],
+                            unit["values_t"][:, b0 + i, :],
+                            start=(b0 + i == 0),
+                            stop=(b0 + i == BLOCKS - 1),
+                        )
 
-        inverse = held.tile([P, KV_HEADS * HEAD_BLOCKS], F32, name="inverse")
-        nc.vector.reciprocal(inverse[:], denominator[:])
-        result = held.tile([P, KV_HEADS * HEAD_BLOCKS, D], F32, name="result")
-        for g in range(KV_HEADS * HEAD_BLOCKS):
-            nc.vector.tensor_scalar_mul(result[:, g, :], numerator[:, g, :], inverse[:, g : g + 1])
-        nc.sync.dma_start(out_blocks, result[:])
+        def combine(unit, sums):
+            z_sum = stats.tile([P, HEAD_BLOCKS], F32, tag="z_sum")
+            z_max = stats.tile([P, HEAD_BLOCKS], F32, tag="z_max")
+            for g in range(HEAD_BLOCKS):
+                nc.vector.tensor_reduce(z_max[:, g : g + 1], sums[g][:, D:], X, MAX)
+                nc.vector.tensor_reduce(z_sum[:, g : g + 1], sums[g][:, D:], X, ADD)
+            weight = stats.tile([P, HEAD_BLOCKS], F32, tag="weight")
+            nc.vector.reciprocal(weight[:], z_max[:])
+            nc.vector.tensor_mul(weight[:], weight[:], z_sum[:])
+            first = unit["a"] * HEAD_BLOCKS
+            for g in range(HEAD_BLOCKS):
+                nc.vector.scalar_tensor_tensor(
+                    numerator[:, first + g, :],
+                    sums[g][:, :D],
+                    weight[:, g : g + 1],
+                    numerator[:, first + g, :],
+                    MULT,
+                    ADD,
+                )
+            nc.vector.tensor_add(
+                denominator[:, first : first + HEAD_BLOCKS], denominator[:, first : first + HEAD_BLOCKS], z_sum[:]
+            )
+
+        def finish(a):
+            first = a * HEAD_BLOCKS
+            inverse = stats.tile([P, HEAD_BLOCKS], F32, tag="inverse")
+            nc.vector.reciprocal(inverse[:], denominator[:, first : first + HEAD_BLOCKS])
+            result = stats.tile([P, HEAD_BLOCKS, D], F32, tag="result")
+            for g in range(HEAD_BLOCKS):
+                nc.vector.tensor_scalar_mul(result[:, g, :], numerator[:, first + g, :], inverse[:, g : g + 1])
+            nc.sync.dma_start(out_blocks[:, first : first + HEAD_BLOCKS, :], result[:])
+
+        units = [(r, a) for r in range(RANKS) for a in range(KV_HEADS)]
+        following = open_unit(*units[0])
+        nc.sync.dma_start(queries[:], q)
+        for step in range(STEPS):
+            look_up(following, step)
+        for u in range(len(units)):
+            unit = following
+            if u + 1 < len(units):
+                following = open_unit(*units[u + 1])
+            sums = [sum_banks.tile([P, D + SPLITS], F32, name="sums%d" % g) for g in range(HEAD_BLOCKS)]
+            for step in range(STEPS):
+                if u + 1 < len(units):
+                    look_up(following, step)
+                attend(unit, sums, step)
+            combine(unit, sums)
+            if unit["r"] == RANKS - 1:
+                finish(unit["a"])

@@ -21,9 +21,9 @@ BLOCKS = L // P
 SPLITS_IN_BLOCK = P // SPLIT
 HEAD_BLOCKS = GROUP // P
 SCORE_BLOCKS = 512 // GROUP
-FLIP_BLOCKS = 512 // D
 
-PIECE = 1024
+PIECE = 512
+PIECE_BLOCKS = PIECE // P
 PIECES = L // PIECE
 STEPS = 2 * PIECES
 STEP_BLOCKS = BLOCKS // STEPS
@@ -49,7 +49,7 @@ def tile_spgqaflashdecodeiris_b_kernel(tc, q, kv, offs, out):
         offsets = held.tile([P, RANKS * L // 16], U16, name="offsets")
         nc.sync.dma_start(offsets[:], offs)
 
-        identity = held.tile([P, P], F32, name="identity")
+        identity = held.tile([P, P], BF16, name="identity")
         make_identity(nc, identity[:])
 
         marks = held.tile([P, BLOCKS, SPLITS], BF16, name="marks")
@@ -84,12 +84,13 @@ def tile_spgqaflashdecodeiris_b_kernel(tc, q, kv, offs, out):
             piece = picked.tile([P, PIECE], F32, tag="piece")
             nc.scalar.activation(piece[:], window[:].indirect(piece_offsets), COPY)
             if step < PIECES:
-                for c0 in range(0, PIECE // P, FLIP_BLOCKS):
-                    flipped = flip_banks.tile([P, FLIP_BLOCKS, D], F32, tag="flipped")
-                    for c in range(FLIP_BLOCKS):
-                        nc.tensor.transpose(flipped[:, c, :], piece[:, (c0 + c) * P : (c0 + c + 1) * P], identity[:])
-                    b0 = i * (PIECE // P) + c0
-                    nc.vector.tensor_copy(unit["values_t"][:, b0 : b0 + FLIP_BLOCKS, :D], flipped[:])
+                values = picked.tile([P, PIECE], BF16, tag="values")
+                nc.vector.tensor_copy(values[:], piece[:])
+                flipped = flip_banks.tile([P, PIECE_BLOCKS, D], BF16, tag="flipped")
+                for c in range(PIECE_BLOCKS):
+                    nc.tensor.transpose(flipped[:, c, :], values[:, c * P : (c + 1) * P], identity[:])
+                b0 = i * PIECE_BLOCKS
+                nc.vector.tensor_copy(unit["values_t"][:, b0 : b0 + PIECE_BLOCKS, :D], flipped[:])
             else:
                 nc.vector.tensor_copy(unit["keys"][:, i * PIECE : (i + 1) * PIECE], piece[:])
 

@@ -49,7 +49,7 @@ def tile_spgqaflashdecodeiris_b_kernel(tc, q, kv, offs, out):
         offsets = held.tile([P, RANKS * L // 16], U16, name="offsets")
         nc.sync.dma_start(offsets[:], offs)
 
-        identity = held.tile([P, P], BF16, name="identity")
+        identity = held.tile([P, P], F32, name="identity")
         make_identity(nc, identity[:])
 
         marks = held.tile([P, BLOCKS, SPLITS], BF16, name="marks")
@@ -84,11 +84,9 @@ def tile_spgqaflashdecodeiris_b_kernel(tc, q, kv, offs, out):
             piece = picked.tile([P, PIECE], F32, tag="piece")
             nc.scalar.activation(piece[:], window[:].indirect(piece_offsets), COPY)
             if step < PIECES:
-                values = picked.tile([P, PIECE], BF16, tag="values")
-                nc.vector.tensor_copy(values[:], piece[:])
-                flipped = flip_banks.tile([P, PIECE_BLOCKS, D], BF16, tag="flipped")
+                flipped = flip_banks.tile([P, PIECE_BLOCKS, D], F32, tag="flipped")
                 for c in range(PIECE_BLOCKS):
-                    nc.tensor.transpose(flipped[:, c, :], values[:, c * P : (c + 1) * P], identity[:])
+                    nc.tensor.transpose(flipped[:, c, :], piece[:, c * P : (c + 1) * P], identity[:])
                 b0 = i * PIECE_BLOCKS
                 nc.vector.tensor_copy(unit["values_t"][:, b0 : b0 + PIECE_BLOCKS, :D], flipped[:])
             else:

@@ -49,7 +49,11 @@ def tile_spgqaflashdecodeiris_b_kernel(tc, q, kv, offs, out):
         offsets = held.tile([P, RANKS * L // 16], U16, name="offsets")
         nc.sync.dma_start(offsets[:], offs)
 
-        identity = held.tile([P, P], F32, name="identity")
+        warm_up = held.tile([P, 1], F32, name="warm_up")
+        nc.vector.memset(warm_up[:], 0.0)
+        nc.scalar.activation(warm_up[:], warm_up[:], EXP)
+
+        identity = held.tile([P, P], BF16, name="identity")
         make_identity(nc, identity[:])
 
         marks = held.tile([P, BLOCKS, SPLITS], BF16, name="marks")
@@ -84,9 +88,11 @@ def tile_spgqaflashdecodeiris_b_kernel(tc, q, kv, offs, out):
             piece = picked.tile([P, PIECE], F32, tag="piece")
             nc.scalar.activation(piece[:], window[:].indirect(piece_offsets), COPY)
             if step < PIECES:
-                flipped = flip_banks.tile([P, PIECE_BLOCKS, D], F32, tag="flipped")
+                values = picked.tile([P, PIECE], BF16, tag="values")
+                nc.vector.tensor_copy(values[:], piece[:])
+                flipped = flip_banks.tile([P, PIECE_BLOCKS, D], BF16, tag="flipped")
                 for c in range(PIECE_BLOCKS):
-                    nc.tensor.transpose(flipped[:, c, :], piece[:, c * P : (c + 1) * P], identity[:])
+                    nc.tensor.transpose(flipped[:, c, :], values[:, c * P : (c + 1) * P], identity[:])
                 b0 = i * PIECE_BLOCKS
                 nc.vector.tensor_copy(unit["values_t"][:, b0 : b0 + PIECE_BLOCKS, :D], flipped[:])
             else:

import math

import concourse.mybir as mybir
from concourse.masks import make_identity

F32, BF16, U16 = mybir.dt.float32, mybir.dt.bfloat16, mybir.dt.uint16
COPY, EXP = mybir.ActivationFunctionType.Copy, mybir.ActivationFunctionType.Exp
MULT, ADD, MAX = mybir.AluOpType.mult, mybir.AluOpType.add, mybir.AluOpType.max
X = mybir.AxisListType.X

P = 128
RANKS = 4
KV_HEADS = 2
GROUP = 256
D = 128
SLOTS = 4096
L = 2048
SPLITS = 32
SPLIT = L // SPLITS
BLOCKS = L // P
SPLITS_IN_BLOCK = P // SPLIT
HEAD_BLOCKS = GROUP // P
SCORE_BLOCKS = 512 // GROUP

PIECE = 512
PIECE_BLOCKS = PIECE // P
PIECES = L // PIECE
STEPS = 2 * PIECES
STEP_BLOCKS = BLOCKS // STEPS

FLOPS = 2 * 2 * (KV_HEADS * GROUP) * (RANKS * L) * D


def tile_spgqaflashdecodeiris_b_kernel(tc, q, kv, offs, out):
    nc = tc.nc
    out_blocks = out.rearrange("(b p) d -> p b d", p=P)

    with (
        tc.tile_pool(name="held", bufs=1) as held,
        tc.tile_pool(name="windows", bufs=5) as windows,
        tc.tile_pool(name="picked", bufs=4) as picked,
        tc.tile_pool(name="operands", bufs=3) as operands,
        tc.tile_pool(name="e_pieces", bufs=6) as e_pieces,
        tc.tile_pool(name="stats", bufs=2) as stats,
        tc.psum_pool(name="score_banks", bufs=4) as score_banks,
        tc.psum_pool(name="flip_banks", bufs=2) as flip_banks,
        tc.psum_pool(name="sum_banks", bufs=1) as sum_banks,
    ):
        offsets = held.tile([P, RANKS * L // 16], U16, name="offsets")
        nc.sync.dma_start(offsets[:], offs)

        warm_up = held.tile([P, 1], F32, name="warm_up")
        nc.vector.memset(warm_up[:], 0.0)
        nc.scalar.activation(warm_up[:], warm_up[:], EXP)

        identity = held.tile([P, P], BF16, name="identity")
        make_identity(nc, identity[:])

        marks = held.tile([P, BLOCKS, SPLITS], BF16, name="marks")
        nc.vector.memset(marks[:], 0.0)
        for b in range(BLOCKS):
            for s in range(SPLITS_IN_BLOCK):
                t = SPLITS_IN_BLOCK * b + s
                nc.vector.memset(marks[s * SPLIT : (s + 1) * SPLIT, b, t : t + 1], 1.0)

        numerator = held.tile([P, KV_HEADS * HEAD_BLOCKS, D], F32, name="numerator")
        denominator = held.tile([P, KV_HEADS * HEAD_BLOCKS], F32, name="denominator")
        nc.vector.memset(numerator[:], 0.0)
        nc.vector.memset(denominator[:], 0.0)
        queries = held.tile([P, KV_HEADS * GROUP], BF16, name="queries")

        def open_unit(r, a):
            value_window = windows.tile([P, SLOTS], F32, tag="window")
            nc.sync.dma_start(value_window[:], kv[r, (KV_HEADS + a) * D : (KV_HEADS + a + 1) * D, :])
            key_window = windows.tile([P, SLOTS], F32, tag="window")
            nc.sync.dma_start(key_window[:], kv[r, a * D : (a + 1) * D, :])
            values_t = operands.tile([P, BLOCKS, D + SPLITS], BF16, tag="values_t")
            nc.vector.tensor_copy(values_t[:, :, D:], marks[:])
            keys = operands.tile([P, L], BF16, tag="keys")
            return {"r": r, "a": a, "value_window": value_window, "key_window": key_window,
                    "values_t": values_t, "keys": keys}

        def look_up(unit, step):
            i = step % PIECES
            first_column = (unit["r"] * L + i * PIECE) // 16
            piece_offsets = offsets[:, first_column : first_column + PIECE // 16]
            window = unit["value_window"] if step < PIECES else unit["key_window"]
            piece = picked.tile([P, PIECE], F32, tag="piece")
            nc.scalar.activation(piece[:], window[:].indirect(piece_offsets), COPY)
            if step < PIECES:
                values = picked.tile([P, PIECE], BF16, tag="values")
                nc.vector.tensor_copy(values[:], piece[:])
                flipped = flip_banks.tile([P, PIECE_BLOCKS, D], BF16, tag="flipped")
                for c in range(PIECE_BLOCKS):
                    nc.tensor.transpose(flipped[:, c, :], values[:, c * P : (c + 1) * P], identity[:])
                b0 = i * PIECE_BLOCKS
                nc.vector.tensor_copy(unit["values_t"][:, b0 : b0 + PIECE_BLOCKS, :D], flipped[:])
            else:
                nc.vector.tensor_copy(unit["keys"][:, i * PIECE : (i + 1) * PIECE], piece[:])

        def attend(unit, sums, step):
            a = unit["a"]
            for b0 in range(step * STEP_BLOCKS, (step + 1) * STEP_BLOCKS, SCORE_BLOCKS):
                scores = score_banks.tile([P, SCORE_BLOCKS, GROUP], F32, tag="scores")
                for i in range(SCORE_BLOCKS):
                    nc.tensor.matmul(
                        scores[:, i, :],
                        unit["keys"][:, (b0 + i) * P : (b0 + i + 1) * P],
                        queries[:, a * GROUP : (a + 1) * GROUP],
                        start=True,
                        stop=True,
                    )
                e_t = e_pieces.tile([P, SCORE_BLOCKS, GROUP], BF16, tag="e_t")
                nc.scalar.activation(e_t[:], scores[:], EXP, scale=1.0 / math.sqrt(D))
                for i in range(SCORE_BLOCKS):
                    for g in range(HEAD_BLOCKS):
                        nc.tensor.matmul(
                            sums[g][:],
                            e_t[:, i, g * P : (g + 1) * P],
                            unit["values_t"][:, b0 + i, :],
                            start=(b0 + i == 0),
                            stop=(b0 + i == BLOCKS - 1),
                        )

        def combine(unit, sums):
            z_sum = stats.tile([P, HEAD_BLOCKS], F32, tag="z_sum")
            z_max = stats.tile([P, HEAD_BLOCKS], F32, tag="z_max")
            for g in range(HEAD_BLOCKS):
                nc.vector.tensor_reduce(z_max[:, g : g + 1], sums[g][:, D:], X, MAX)
                nc.vector.tensor_reduce(z_sum[:, g : g + 1], sums[g][:, D:], X, ADD)
            weight = stats.tile([P, HEAD_BLOCKS], F32, tag="weight")
            nc.vector.reciprocal(weight[:], z_max[:])
            nc.vector.tensor_mul(weight[:], weight[:], z_sum[:])
            first = unit["a"] * HEAD_BLOCKS
            for g in range(HEAD_BLOCKS):
                nc.vector.scalar_tensor_tensor(
                    numerator[:, first + g, :],
                    sums[g][:, :D],
                    weight[:, g : g + 1],
                    numerator[:, first + g, :],
                    MULT,
                    ADD,
                )
            nc.vector.tensor_add(
                denominator[:, first : first + HEAD_BLOCKS], denominator[:, first : first + HEAD_BLOCKS], z_sum[:]
            )

        def finish(a):
            first = a * HEAD_BLOCKS
            inverse = stats.tile([P, HEAD_BLOCKS], F32, tag="inverse")
            nc.vector.reciprocal(inverse[:], denominator[:, first : first + HEAD_BLOCKS])
            result = stats.tile([P, HEAD_BLOCKS, D], F32, tag="result")
            for g in range(HEAD_BLOCKS):
                nc.vector.tensor_scalar_mul(result[:, g, :], numerator[:, first + g, :], inverse[:, g : g + 1])
            nc.sync.dma_start(out_blocks[:, first : first + HEAD_BLOCKS, :], result[:])

        units = [(r, a) for r in range(RANKS) for a in range(KV_HEADS)]
        following = open_unit(*units[0])
        nc.sync.dma_start(queries[:], q)
        for step in range(STEPS):
            look_up(following, step)
        for u in range(len(units)):
            unit = following
            if u + 1 < len(units):
                following = open_unit(*units[u + 1])
            sums = [sum_banks.tile([P, D + SPLITS], F32, name="sums%d" % g) for g in range(HEAD_BLOCKS)]
            for step in range(STEPS):
                if u + 1 < len(units):
                    look_up(following, step)
                attend(unit, sums, step)
            combine(unit, sums)
            if unit["r"] == RANKS - 1:
                finish(unit["a"])
